import numpy as np
import ml_dtypes


def mxq(x, axis, fmt="e4m3"):
    dtype, down = {"e4m3": (ml_dtypes.float8_e4m3fn, 7), "e5m2": (ml_dtypes.float8_e5m2, 14)}[fmt]
    v = np.moveaxis(np.asarray(x, np.float32).astype(ml_dtypes.bfloat16).astype(np.float64), axis, -1)
    blocks = v.reshape(v.shape[:-1] + (-1, 32))
    amax = np.abs(blocks).max(-1, keepdims=True)
    byte = np.maximum(np.where(amax > 0, np.frexp(amax)[1] - 1 + 127, 0) - down, 1)
    scale = np.exp2(byte - 127.0)
    codes = (blocks / scale).astype(np.float32).astype(dtype).astype(np.float64)
    return np.moveaxis((codes * scale).reshape(v.shape), -1, axis)


WIDE = False


def mx_kscale(k):
    if not WIDE:
        return np.ones(k)
    levels = np.array([10, -10, 5, -5, 0])
    a = np.random.permutation(np.resize(levels, k // 512 * 4)).reshape(k // 512, 4)
    idx = np.arange(k)
    return np.exp2(a[idx // 512, idx % 128 // 32])


BF16 = ml_dtypes.bfloat16


def bf(x):
    return np.asarray(x, np.float32).astype(BF16)


def f64(x):
    return np.asarray(x).astype(np.float64)


Nc, Ns, Nt, d_h, BS = 64, 8, 16, 128, 64
I, J = Ns * Nt, Nc * Nt


def setup_inputs():
    s = mx_kscale(J)
    Ac = (np.random.random((Ns, Nc)) < 3.2 / Ns).astype(np.float64)
    Ac[np.random.randint(0, Ns, Nc), np.arange(Nc)] = 1.0
    Ac[np.arange(Ns), np.random.randint(0, Nc, Ns)] = 1.0
    As = (np.random.random((Ns, Ns)) < 0.05).astype(np.float64)
    AA = np.dot(np.dot(As, As), Ac) + np.dot(As, Ac) + Ac
    AA = (AA != 0).astype(np.float64)
    AA_mask = np.tile(AA, (Nt, Nt))
    g = 1.0 / np.sqrt(0.5 * J * AA.mean())
    GCW = np.random.standard_normal((I, J)) * g * s[None, :]
    GCB = np.random.standard_normal((I, d_h)) * 0.5
    h = np.random.standard_normal((BS, Nc, Nt, d_h)) / s.reshape(Nt, Nc).T[None, :, :, None]
    e = np.random.standard_normal(1) * 0.1
    return {"h": bf(h), "e": bf(e), "AA_mask": bf(AA_mask), "GCW": bf(GCW), "GCB": bf(GCB)}


def reference(h, e, AA_mask, GCW, GCB):
    bs = h.shape[0]
    A = np.maximum(f64(AA_mask) * f64(GCW), 0.0)
    x = np.transpose(f64(h), (0, 2, 1, 3)).reshape(bs, Nt * Nc, d_h)
    x = np.maximum((mxq(A, 1, "e4m3") @ mxq(x, 1, "e4m3")) + f64(GCB), 0.0)
    x = x.reshape(bs, Nt, Ns, d_h)
    x = np.transpose(x, (0, 2, 1, 3))
    return x

@@ -1,0 +1,225 @@
+from contextlib import ExitStack
+
+import concourse.mybir as mybir
+from concourse.masks import make_identity
+
+BF16 = mybir.dt.bfloat16
+F32 = mybir.dt.float32
+U32 = mybir.dt.uint32
+U8 = mybir.dt.uint8
+I32 = mybir.dt.int32
+FP8X4 = mybir.dt.float8_e4m3fn_x4
+ALU = mybir.AluOpType
+ACT = mybir.ActivationFunctionType
+
+P = 128
+FLOPS = 2 * 64 * 128 * 1024 * 128
+PINNED = True
+NG = 8
+
+
+def tile_gcnfast_t_kernel(tc, h, e, AA_mask, GCW, GCB, out):
+    nc = tc.nc
+    with ExitStack() as ctx:
+        if PINNED:
+            ctx.enter_context(tc.manual_schedule())
+        const = ctx.enter_context(tc.tile_pool(name="const", bufs=1))
+        rawp = ctx.enter_context(tc.tile_pool(name="rawp", bufs=1))
+        grpp = ctx.enter_context(tc.tile_pool(name="grpp", bufs=6))
+        codp = ctx.enter_context(tc.tile_pool(name="codp", bufs=8))
+        yp = ctx.enter_context(tc.tile_pool(name="yp", bufs=8))
+        psum = ctx.enter_context(tc.psum_pool(name="psum", bufs=8))
+
+        hv = h.rearrange("b c t d -> (b c t d)").rearrange("(s m r) -> m s r", m=P, r=2048)
+        ov = out.rearrange("b s t d -> (b s t d)").rearrange("(s m r) -> m s r", m=P, r=256)
+
+        ident = const.tile([P, P], BF16, name="ident")
+        perm = const.tile([P, P], BF16, name="perm")
+        sel = const.tile([P, 2, 2, 64], BF16, name="sel")
+        gcw = const.tile([P, 1024], BF16, name="gcw")
+        msk = const.tile([P, 1024], BF16, name="msk")
+        gcb = const.tile([P, P], BF16, name="gcb")
+        pa = const.tile([P, 1024], BF16, name="pa")
+        pb = const.tile([P, 1024], BF16, name="pb")
+        ga = const.tile([P, 4096], BF16, name="ga", align_bytes=64)
+        a_codes = const.tile([P, 1024], U32, name="a_codes", align_bytes=64)
+        a_scl = const.tile([P, 1024], U8, name="a_scl", align_bytes=64)
+        bias = const.tile([P, 2, P], F32, name="bias")
+        raw = [rawp.tile([P, 4, 2048], BF16, name="raw%d" % g) for g in range(NG)]
+
+        grp = {}
+        codes = {}
+        scl = {}
+        acc = {}
+        ys = {}
+
+        def load(g, s0, s1):
+            nc.sync.dma_start(out=raw[g][:, s0:s1, :], in_=hv[:, 4 * g + s0 : 4 * g + s1, :])
+
+        def views(g, q):
+            if (g, q) not in grp:
+                grp[(g, q)] = grpp.tile([P, 2048], BF16, name="grp", tag="grp", align_bytes=64)
+            t3, t0 = q // 2, q % 2
+            rv = raw[g][:].rearrange(
+                "p s (a j e c i) -> p s a j e c i", a=2, j=4, e=2, c=32, i=4
+            )
+            src = rv[:, :, t3, :, t0, :, :].rearrange("p s j c i -> p s c j i")
+            dst = grp[(g, q)][:].rearrange("p (s c i j) -> p s c j i", s=4, c=32, i=4, j=4)
+            return src, dst
+
+        def regroup_v(g, q):
+            src, dst = views(g, q)
+            nc.vector.tensor_copy(out=dst, in_=src)
+
+        def regroup_v_piece(g, q, s):
+            src, dst = views(g, q)
+            nc.vector.tensor_copy(out=dst[:, s], in_=src[:, s])
+
+        def regroup_s_piece(g, q, s):
+            src, dst = views(g, q)
+            nc.scalar.copy(out=dst[:, s], in_=src[:, s])
+
+        def regroup_s(g, q):
+            for s in range(4):
+                regroup_s_piece(g, q, s)
+
+        def quant_mm(g, q):
+            codes[(g, q)] = codp.tile([P, 512], U32, name="codes", tag="codes", align_bytes=64)
+            scl[(g, q)] = codp.tile([P, 512], U8, name="scl", tag="scl", align_bytes=64)
+            nc.vector.quantize_mx(
+                out=codes[(g, q)][:].bitcast(FP8X4), scales=scl[(g, q)][:], in_=grp[(g, q)][:]
+            )
+            for l in range(2):
+                if q == 0:
+                    acc[(g, l)] = psum.tile([P, 512], F32, name="acc", tag="bank")
+                col = (q * 2 + l) * P
+                nc.tensor.matmul_mx(
+                    out=acc[(g, l)][:],
+                    lhsT=a_codes[:, col : col + P].bitcast(FP8X4),
+                    lhsT_scale=a_scl[:, col : col + P],
+                    rhs=codes[(g, q)][:].bitcast(FP8X4),
+                    rhs_scale=scl[(g, q)][:],
+                    start=(q == 0),
+                    stop=(q == 3),
+                )
+
+        def add(g, l):
+            if g not in ys:
+                ys[g] = yp.tile([P, 4, 2, P], F32, name="y", tag="y")
+            nc.vector.tensor_tensor(
+                out=ys[g][:, :, l, :],
+                in0=acc[(g, l)][:].rearrange("p (s d) -> p s d", s=4),
+                in1=bias[:, l, :].unsqueeze(1).to_broadcast([P, 4, P]),
+                op=ALU.add,
+            )
+
+        def relu_store(g):
+            yf = ys[g][:].rearrange("p s l d -> p (s l d)")
+            nc.scalar.activation(out=yf, in_=yf, func=ACT.Relu)
+            nc.sync.dma_start(
+                out=ov[:, 4 * g : 4 * g + 4, :], in_=ys[g][:].rearrange("p s l d -> p s (l d)")
+            )
+
+        nc.vector.memset(ga[:].bitcast(I32), 0)
+        make_identity(nc, ident[:])
+        load(0, 0, 1)
+        nc.sync.dma_start(out=gcw[:], in_=GCW)
+        nc.sync.dma_start(out=msk[:], in_=AA_mask)
+        nc.sync.dma_start(out=gcb[:], in_=GCB)
+        for s in range(1, 4):
+            load(0, s, s + 1)
+        for g in range(1, NG):
+            load(g, 0, 2)
+            load(g, 2, 4)
+
+        nc.vector.tensor_copy(
+            out=perm[:].rearrange("p (l s h) -> p l s h", l=2, s=8, h=8),
+            in_=ident[:].rearrange("p (h l s) -> p l s h", h=8, l=2, s=8),
+        )
+        nc.vector.tensor_copy(
+            out=sel[:],
+            in_=perm[:].rearrange("p (l m) -> p l m", l=2).unsqueeze(2).to_broadcast([P, 2, 2, 64]),
+        )
+
+        def pieces(s):
+            regroup_v_piece(0, 0, s)
+            regroup_v_piece(0, 2, s)
+            regroup_s_piece(0, 1, s)
+            regroup_s_piece(0, 3, s)
+
+        pieces(0)
+        nc.vector.tensor_tensor(out=pa[:], in0=gcw[:], in1=msk[:], op=ALU.mult)
+        pav = pa[:].rearrange("p (u e c) -> p u e c", u=8, e=2, c=64)
+        pbv = pb[:].rearrange("p (u e c) -> p u e c", u=8, e=2, c=64)
+        for ee in range(2):
+            nc.vector.tensor_copy(out=pbv[:, :, ee, :], in_=pav[:, :, 1 - ee, :])
+        psx = []
+        psz = []
+        for t3 in range(2):
+            px = psum.tile([P, 4, P], BF16, name="px", tag="bank")
+            for j in range(4):
+                u = 4 * t3 + j
+                nc.tensor.transpose(out=px[:, j, :], in_=pa[:, P * u : P * u + P], identity=perm[:])
+            psx.append(px)
+        for t3 in range(2):
+            pz = psum.tile([P, 4, P], BF16, name="pz", tag="bank")
+            for j in range(4):
+                u = 4 * t3 + j
+                nc.tensor.transpose(out=pz[:, j, :], in_=pb[:, P * u : P * u + P], identity=perm[:])
+            psz.append(pz)
+        bps = psum.tile([P, 2, P], F32, name="bps", tag="bank")
+        for l in range(2):
+            nc.tensor.matmul(
+                out=bps[:, l, :],
+                lhsT=sel[:, l, :, :].rearrange("p b m -> p (b m)"),
+                rhs=gcb[:],
+                start=True,
+                stop=True,
+            )
+        pieces(1)
+        gav = ga[:].rearrange("p (q l b m j) -> p q l b m j", q=4, l=2, b=2, m=64, j=4)
+
+        def pview(ps, lo, hi):
+            return ps[lo:hi].rearrange("p j (l m) -> p l m j", l=2)
+
+        for t3 in range(2):
+            nc.vector.tensor_scalar_max(
+                out=gav[0:64, 2 * t3, :, 0, :, :], in0=pview(psx[t3], 0, 64), scalar1=0.0
+            )
+            nc.scalar.activation(
+                out=gav[64:128, 2 * t3 + 1, :, 1, :, :], in_=pview(psx[t3], 64, 128), func=ACT.Relu
+            )
+        pieces(2)
+        for t3 in range(2):
+            nc.vector.tensor_scalar_max(
+                out=gav[0:64, 2 * t3 + 1, :, 0, :, :], in0=pview(psz[t3], 0, 64), scalar1=0.0
+            )
+            nc.scalar.activation(
+                out=gav[64:128, 2 * t3, :, 1, :, :], in_=pview(psz[t3], 64, 128), func=ACT.Relu
+            )
+        nc.vector.tensor_copy(out=bias[:], in_=bps[:])
+        pieces(3)
+        nc.vector.quantize_mx(out=a_codes[:].bitcast(FP8X4), scales=a_scl[:], in_=ga[:])
+        quant_mm(0, 0)
+        quant_mm(0, 1)
+        quant_mm(0, 2)
+
+        for g in range(1, NG):
+            if g >= 2:
+                relu_store(g - 2)
+            regroup_v(g, 0)
+            regroup_s(g, 1)
+            quant_mm(g - 1, 3)
+            regroup_v(g, 2)
+            quant_mm(g, 0)
+            add(g - 1, 0)
+            regroup_s(g, 3)
+            quant_mm(g, 1)
+            add(g - 1, 1)
+            quant_mm(g, 2)
+
+        relu_store(NG - 2)
+        quant_mm(NG - 1, 3)
+        add(NG - 1, 0)
+        add(NG - 1, 1)
+        relu_store(NG - 1)

@@ -14,21 +14,26 @@ ACT = mybir.ActivationFunctionType
 
 P = 128
 FLOPS = 2 * 64 * 128 * 1024 * 128
-PINNED = True
-NG = 8
+UNITS = [(0, 4), (4, 4), (8, 4), (12, 4), (16, 4), (20, 4), (24, 4), (28, 2), (30, 2)]
+LOADS = [(1, 2), (2, 3), (3, 4)] + [(a, a + 2) for a in range(4, 32, 2)]
+VSHARE = [(2, 2, 2, 2)] + [(2, 2, 2, 1)] * 6 + [(1, 1, 1, 1)] * 2
+G_UNITS = ()
+G_PAIRS = 0
+PE_UNITS = ()
 
 
 def tile_gcnfast_t_kernel(tc, h, e, AA_mask, GCW, GCB, out):
     nc = tc.nc
+    nu = len(UNITS)
     with ExitStack() as ctx:
-        if PINNED:
-            ctx.enter_context(tc.manual_schedule())
+        ctx.enter_context(tc.manual_schedule())
         const = ctx.enter_context(tc.tile_pool(name="const", bufs=1))
         rawp = ctx.enter_context(tc.tile_pool(name="rawp", bufs=1))
-        grpp = ctx.enter_context(tc.tile_pool(name="grpp", bufs=6))
-        codp = ctx.enter_context(tc.tile_pool(name="codp", bufs=8))
+        grpp = ctx.enter_context(tc.tile_pool(name="grpp", bufs=3))
+        codp = ctx.enter_context(tc.tile_pool(name="codp", bufs=3))
         yp = ctx.enter_context(tc.tile_pool(name="yp", bufs=8))
-        psum = ctx.enter_context(tc.psum_pool(name="psum", bufs=8))
+        psa = ctx.enter_context(tc.psum_pool(name="psa", bufs=6))
+        psb = ctx.enter_context(tc.psum_pool(name="psb", bufs=2))
 
         hv = h.rearrange("b c t d -> (b c t d)").rearrange("(s m r) -> m s r", m=P, r=2048)
         ov = out.rearrange("b s t d -> (b s t d)").rearrange("(s m r) -> m s r", m=P, r=256)
@@ -45,92 +50,129 @@ def tile_gcnfast_t_kernel(tc, h, e, AA_mask, GCW, GCB, out):
         a_codes = const.tile([P, 1024], U32, name="a_codes", align_bytes=64)
         a_scl = const.tile([P, 1024], U8, name="a_scl", align_bytes=64)
         bias = const.tile([P, 2, P], F32, name="bias")
-        raw = [rawp.tile([P, 4, 2048], BF16, name="raw%d" % g) for g in range(NG)]
+        raw = rawp.tile([P, 32, 2048], BF16, name="raw")
 
         grp = {}
-        codes = {}
-        scl = {}
         acc = {}
         ys = {}
 
-        def load(g, s0, s1):
-            nc.sync.dma_start(out=raw[g][:, s0:s1, :], in_=hv[:, 4 * g + s0 : 4 * g + s1, :])
-
-        def views(g, q):
-            if (g, q) not in grp:
-                grp[(g, q)] = grpp.tile([P, 2048], BF16, name="grp", tag="grp", align_bytes=64)
+        def views(u, q):
+            s0, n = UNITS[u]
             t3, t0 = q // 2, q % 2
-            rv = raw[g][:].rearrange(
+            if (u, t3) not in grp:
+                grp[(u, t3)] = grpp.tile([P, 1024 * n], BF16, name="grp", tag="grp", align_bytes=64)
+            rv = raw[:, s0 : s0 + n, :].rearrange(
                 "p s (a j e c i) -> p s a j e c i", a=2, j=4, e=2, c=32, i=4
             )
             src = rv[:, :, t3, :, t0, :, :].rearrange("p s j c i -> p s c j i")
-            dst = grp[(g, q)][:].rearrange("p (s c i j) -> p s c j i", s=4, c=32, i=4, j=4)
+            dst = grp[(u, t3)][:, 512 * n * t0 : 512 * n * (t0 + 1)].rearrange(
+                "p (s c i j) -> p s c j i", s=n, c=32, i=4, j=4
+            )
             return src, dst
 
-        def regroup_v(g, q):
-            src, dst = views(g, q)
-            nc.vector.tensor_copy(out=dst, in_=src)
+        def regroup_v(u, q, a, b):
+            src, dst = views(u, q)
+            if b - a == 1:
+                nc.vector.tensor_copy(out=dst[:, a], in_=src[:, a])
+            elif b > a:
+                nc.vector.tensor_copy(out=dst[:, a:b], in_=src[:, a:b])
 
-        def regroup_v_piece(g, q, s):
-            src, dst = views(g, q)
-            nc.vector.tensor_copy(out=dst[:, s], in_=src[:, s])
+        def regroup_s(u, q, a, b):
+            src, dst = views(u, q)
+            for s in range(a, b):
+                nc.scalar.copy(out=dst[:, s], in_=src[:, s])
 
-        def regroup_s_piece(g, q, s):
-            src, dst = views(g, q)
-            nc.scalar.copy(out=dst[:, s], in_=src[:, s])
-
-        def regroup_s(g, q):
-            for s in range(4):
-                regroup_s_piece(g, q, s)
-
-        def quant_mm(g, q):
-            codes[(g, q)] = codp.tile([P, 512], U32, name="codes", tag="codes", align_bytes=64)
-            scl[(g, q)] = codp.tile([P, 512], U8, name="scl", tag="scl", align_bytes=64)
-            nc.vector.quantize_mx(
-                out=codes[(g, q)][:].bitcast(FP8X4), scales=scl[(g, q)][:], in_=grp[(g, q)][:]
-            )
-            for l in range(2):
-                if q == 0:
-                    acc[(g, l)] = psum.tile([P, 512], F32, name="acc", tag="bank")
-                col = (q * 2 + l) * P
-                nc.tensor.matmul_mx(
-                    out=acc[(g, l)][:],
-                    lhsT=a_codes[:, col : col + P].bitcast(FP8X4),
-                    lhsT_scale=a_scl[:, col : col + P],
-                    rhs=codes[(g, q)][:].bitcast(FP8X4),
-                    rhs_scale=scl[(g, q)][:],
-                    start=(q == 0),
-                    stop=(q == 3),
+        def regroup_pe(u):
+            s0, n = UNITS[u]
+            views(u, 3)
+            bank = psb.tile([P, 2, P, 4], BF16, name="idb", tag="idb")
+            for j in range(4):
+                t = 8 + 2 * j + 1
+                nc.tensor.matmul(
+                    out=bank[:, :, :, j],
+                    lhsT=ident[:],
+                    rhs=raw[:, s0 + 2 : s0 + 4, P * t : P * t + P],
+                    start=True,
+                    stop=True,
                 )
+            nc.scalar.copy(
+                out=grp[(u, 1)][:, 512 * n + 1024 : 512 * n + 2048],
+                in_=bank[:].rearrange("p s d j -> p (s d j)"),
+            )
 
-        def add(g, l):
-            if g not in ys:
-                ys[g] = yp.tile([P, 4, 2, P], F32, name="y", tag="y")
+        def regroup(u, q):
+            n = UNITS[u][1]
+            k = VSHARE[u][q]
+            regroup_v(u, q, 0, k)
+            if q == 3 and u in PE_UNITS:
+                regroup_s(u, q, k, 2)
+                regroup_pe(u)
+            else:
+                regroup_s(u, q, k, n)
+
+        def quant_mm(u, t3):
+            n = UNITS[u][1]
+            w = P * n
+            cod = codp.tile([P, 2 * w], U32, name="cod", tag="cod", align_bytes=64)
+            scl = codp.tile([P, 2 * w], U8, name="scl", tag="scl", align_bytes=64)
+            nc.vector.quantize_mx(out=cod[:].bitcast(FP8X4), scales=scl[:], in_=grp[(u, t3)][:])
+            for t0 in range(2):
+                q = 2 * t3 + t0
+                for l in range(2):
+                    if q == 0:
+                        acc[(u, l)] = psa.tile([P, w], F32, name="acc", tag="acc")
+                    col = (q * 2 + l) * P
+                    nc.tensor.matmul_mx(
+                        out=acc[(u, l)][:],
+                        lhsT=a_codes[:, col : col + P].bitcast(FP8X4),
+                        lhsT_scale=a_scl[:, col : col + P],
+                        rhs=cod[:, w * t0 : w * t0 + w].bitcast(FP8X4),
+                        rhs_scale=scl[:, w * t0 : w * t0 + w],
+                        start=(q == 0),
+                        stop=(q == 3),
+                    )
+
+        def add(u, l):
+            n = UNITS[u][1]
+            if u not in ys:
+                ys[u] = yp.tile([P, n, 2, P], F32, name="y", tag="y")
             nc.vector.tensor_tensor(
-                out=ys[g][:, :, l, :],
-                in0=acc[(g, l)][:].rearrange("p (s d) -> p s d", s=4),
-                in1=bias[:, l, :].unsqueeze(1).to_broadcast([P, 4, P]),
+                out=ys[u][:, :, l, :],
+                in0=acc[(u, l)][:].rearrange("p (s d) -> p s d", s=n),
+                in1=bias[:, l, :].unsqueeze(1).to_broadcast([P, n, P]),
                 op=ALU.add,
             )
 
-        def relu_store(g):
-            yf = ys[g][:].rearrange("p s l d -> p (s l d)")
-            nc.scalar.activation(out=yf, in_=yf, func=ACT.Relu)
+        def relu(u):
+            n = UNITS[u][1]
+            yf = ys[u][:].rearrange("p s l d -> p (s l d)")
+            g = G_PAIRS if u in G_UNITS else 0
+            if g > 0:
+                nc.gpsimd.tensor_scalar(
+                    out=yf[:, 0 : 256 * g], in0=yf[:, 0 : 256 * g],
+                    scalar1=0.0, scalar2=0.0, op0=ALU.max, op1=ALU.add,
+                )
+            if g < n:
+                nc.scalar.activation(out=yf[:, 256 * g :], in_=yf[:, 256 * g :], func=ACT.Relu)
+
+        def relu_half(u, l):
+            nc.scalar.activation(out=ys[u][:, :, l, :], in_=ys[u][:, :, l, :], func=ACT.Relu)
+
+        def store(u):
+            s0, n = UNITS[u]
             nc.sync.dma_start(
-                out=ov[:, 4 * g : 4 * g + 4, :], in_=ys[g][:].rearrange("p s l d -> p s (l d)")
+                out=ov[:, s0 : s0 + n, :], in_=ys[u][:].rearrange("p s l d -> p s (l d)")
             )
 
         nc.vector.memset(ga[:].bitcast(I32), 0)
         make_identity(nc, ident[:])
-        load(0, 0, 1)
         nc.sync.dma_start(out=gcw[:], in_=GCW)
         nc.sync.dma_start(out=msk[:], in_=AA_mask)
         nc.sync.dma_start(out=gcb[:], in_=GCB)
-        for s in range(1, 4):
-            load(0, s, s + 1)
-        for g in range(1, NG):
-            load(g, 0, 2)
-            load(g, 2, 4)
+        nc.sync.dma_start(out=raw[:, 0, 0:1024], in_=hv[:, 0, 0:1024])
+        nc.sync.dma_start(out=raw[:, 0, 1024:2048], in_=hv[:, 0, 1024:2048])
+        for a, b in LOADS:
+            nc.sync.dma_start(out=raw[:, a:b, :], in_=hv[:, a:b, :])
 
         nc.vector.tensor_copy(
             out=perm[:].rearrange("p (l s h) -> p l s h", l=2, s=8, h=8),
@@ -142,12 +184,11 @@ def tile_gcnfast_t_kernel(tc, h, e, AA_mask, GCW, GCB, out):
         )
 
         def pieces(s):
-            regroup_v_piece(0, 0, s)
-            regroup_v_piece(0, 2, s)
-            regroup_s_piece(0, 1, s)
-            regroup_s_piece(0, 3, s)
+            regroup_v(0, 0, s, s + 1)
+            regroup_s(0, 1, s, s + 1)
+            regroup_v(0, 2, s, s + 1)
+            regroup_s(0, 3, s, s + 1)
 
-        pieces(0)
         nc.vector.tensor_tensor(out=pa[:], in0=gcw[:], in1=msk[:], op=ALU.mult)
         pav = pa[:].rearrange("p (u e c) -> p u e c", u=8, e=2, c=64)
         pbv = pb[:].rearrange("p (u e c) -> p u e c", u=8, e=2, c=64)
@@ -156,18 +197,18 @@ def tile_gcnfast_t_kernel(tc, h, e, AA_mask, GCW, GCB, out):
         psx = []
         psz = []
         for t3 in range(2):
-            px = psum.tile([P, 4, P], BF16, name="px", tag="bank")
+            px = psa.tile([P, 4, P], BF16, name="px", tag="acc")
             for j in range(4):
                 u = 4 * t3 + j
                 nc.tensor.transpose(out=px[:, j, :], in_=pa[:, P * u : P * u + P], identity=perm[:])
             psx.append(px)
         for t3 in range(2):
-            pz = psum.tile([P, 4, P], BF16, name="pz", tag="bank")
+            pz = psa.tile([P, 4, P], BF16, name="pz", tag="acc")
             for j in range(4):
                 u = 4 * t3 + j
                 nc.tensor.transpose(out=pz[:, j, :], in_=pb[:, P * u : P * u + P], identity=perm[:])
             psz.append(pz)
-        bps = psum.tile([P, 2, P], F32, name="bps", tag="bank")
+        bps = psb.tile([P, 2, P], F32, name="bps", tag="idb")
         for l in range(2):
             nc.tensor.matmul(
                 out=bps[:, l, :],
@@ -176,50 +217,55 @@ def tile_gcnfast_t_kernel(tc, h, e, AA_mask, GCW, GCB, out):
                 start=True,
                 stop=True,
             )
-        pieces(1)
         gav = ga[:].rearrange("p (q l b m j) -> p q l b m j", q=4, l=2, b=2, m=64, j=4)
 
         def pview(ps, lo, hi):
             return ps[lo:hi].rearrange("p j (l m) -> p l m j", l=2)
 
-        for t3 in range(2):
+        def evac(ps, t3, qlo, qhi):
             nc.vector.tensor_scalar_max(
-                out=gav[0:64, 2 * t3, :, 0, :, :], in0=pview(psx[t3], 0, 64), scalar1=0.0
+                out=gav[0:64, 2 * t3 + qlo, :, 0, :, :], in0=pview(ps[t3], 0, 64), scalar1=0.0
             )
             nc.scalar.activation(
-                out=gav[64:128, 2 * t3 + 1, :, 1, :, :], in_=pview(psx[t3], 64, 128), func=ACT.Relu
+                out=gav[64:128, 2 * t3 + qhi, :, 1, :, :], in_=pview(ps[t3], 64, 128), func=ACT.Relu
             )
+
+        pieces(0)
+        evac(psx, 0, 0, 1)
+        pieces(1)
+        evac(psx, 1, 0, 1)
+        evac(psz, 0, 1, 0)
         pieces(2)
-        for t3 in range(2):
-            nc.vector.tensor_scalar_max(
-                out=gav[0:64, 2 * t3 + 1, :, 0, :, :], in0=pview(psz[t3], 0, 64), scalar1=0.0
-            )
-            nc.scalar.activation(
-                out=gav[64:128, 2 * t3, :, 1, :, :], in_=pview(psz[t3], 64, 128), func=ACT.Relu
-            )
+        evac(psz, 1, 1, 0)
         nc.vector.tensor_copy(out=bias[:], in_=bps[:])
         pieces(3)
         nc.vector.quantize_mx(out=a_codes[:].bitcast(FP8X4), scales=a_scl[:], in_=ga[:])
         quant_mm(0, 0)
-        quant_mm(0, 1)
-        quant_mm(0, 2)
 
-        for g in range(1, NG):
-            if g >= 2:
-                relu_store(g - 2)
-            regroup_v(g, 0)
-            regroup_s(g, 1)
-            quant_mm(g - 1, 3)
-            regroup_v(g, 2)
-            quant_mm(g, 0)
-            add(g - 1, 0)
-            regroup_s(g, 3)
-            quant_mm(g, 1)
-            add(g - 1, 1)
-            quant_mm(g, 2)
+        for u in range(1, nu):
+            regroup(u, 0)
+            regroup(u, 1)
+            if u == nu - 1:
+                regroup(u, 2)
+                regroup(u, 3)
+            if u >= 2:
+                add(u - 2, 0)
+                add(u - 2, 1)
+                relu(u - 2)
+                store(u - 2)
+            quant_mm(u - 1, 1)
+            if u < nu - 1:
+                regroup(u, 2)
+                regroup(u, 3)
+            quant_mm(u, 0)
 
-        relu_store(NG - 2)
-        quant_mm(NG - 1, 3)
-        add(NG - 1, 0)
-        add(NG - 1, 1)
-        relu_store(NG - 1)
+        quant_mm(nu - 1, 1)
+        add(nu - 2, 0)
+        add(nu - 2, 1)
+        relu(nu - 2)
+        store(nu - 2)
+        add(nu - 1, 0)
+        relu_half(nu - 1, 0)
+        add(nu - 1, 1)
+        relu_half(nu - 1, 1)
+        store(nu - 1)

@@ -16,9 +16,9 @@ P = 128
 FLOPS = 2 * 64 * 128 * 1024 * 128
 UNITS = [(0, 4), (4, 4), (8, 4), (12, 4), (16, 4), (20, 4), (24, 4), (28, 2), (30, 2)]
 LOADS = [(1, 2), (2, 3), (3, 4)] + [(a, a + 2) for a in range(4, 32, 2)]
-VSHARE = [(2, 2, 2, 2)] + [(2, 2, 2, 1)] * 6 + [(1, 1, 1, 1)] * 2
-G_UNITS = ()
-G_PAIRS = 0
+VSHARE = [(2, 2, 2, 2)] + [(2, 2, 2, 1), (2, 1, 2, 1)] * 3 + [(1, 1, 1, 1)] * 2
+G_UNITS = (0, 1, 2, 3, 4, 5)
+G_PAIRS = 3
 PE_UNITS = ()
 
 

@@ -16,10 +16,8 @@ P = 128
 FLOPS = 2 * 64 * 128 * 1024 * 128
 UNITS = [(0, 4), (4, 4), (8, 4), (12, 4), (16, 4), (20, 4), (24, 4), (28, 2), (30, 2)]
 LOADS = [(1, 2), (2, 3), (3, 4)] + [(a, a + 2) for a in range(4, 32, 2)]
-VSHARE = [(2, 2, 2, 2)] + [(2, 2, 2, 1), (2, 1, 2, 1)] * 3 + [(1, 1, 1, 1)] * 2
-G_UNITS = (0, 1, 2, 3, 4, 5)
-G_PAIRS = 3
-PE_UNITS = ()
+VSHARE = [(0, 0, 0, 0)] + [(2, 2, 2, 1)] * 6 + [(1, 1, 1, 1)] * 2
+V_HEAD = [(0, 2), (0, 2), (0, 2), (0, 2)]
 
 
 def tile_gcnfast_t_kernel(tc, h, e, AA_mask, GCW, GCB, out):
@@ -29,11 +27,11 @@ def tile_gcnfast_t_kernel(tc, h, e, AA_mask, GCW, GCB, out):
         ctx.enter_context(tc.manual_schedule())
         const = ctx.enter_context(tc.tile_pool(name="const", bufs=1))
         rawp = ctx.enter_context(tc.tile_pool(name="rawp", bufs=1))
-        grpp = ctx.enter_context(tc.tile_pool(name="grpp", bufs=3))
+        grpp = ctx.enter_context(tc.tile_pool(name="grpp", bufs=4))
         codp = ctx.enter_context(tc.tile_pool(name="codp", bufs=3))
         yp = ctx.enter_context(tc.tile_pool(name="yp", bufs=8))
         psa = ctx.enter_context(tc.psum_pool(name="psa", bufs=6))
-        psb = ctx.enter_context(tc.psum_pool(name="psb", bufs=2))
+        psb = ctx.enter_context(tc.psum_pool(name="psb", bufs=1))
 
         hv = h.rearrange("b c t d -> (b c t d)").rearrange("(s m r) -> m s r", m=P, r=2048)
         ov = out.rearrange("b s t d -> (b s t d)").rearrange("(s m r) -> m s r", m=P, r=256)
@@ -44,9 +42,10 @@ def tile_gcnfast_t_kernel(tc, h, e, AA_mask, GCW, GCB, out):
         gcw = const.tile([P, 1024], BF16, name="gcw")
         msk = const.tile([P, 1024], BF16, name="msk")
         gcb = const.tile([P, P], BF16, name="gcb")
-        pa = const.tile([P, 1024], BF16, name="pa")
-        pb = const.tile([P, 1024], BF16, name="pb")
-        ga = const.tile([P, 4096], BF16, name="ga", align_bytes=64)
+        pa2 = const.tile([P, 16, 2, 64], BF16, name="pa2")
+        gd = const.tile([P, 2048], BF16, name="gd", align_bytes=64)
+        cd = const.tile([P, 512], U32, name="cd", align_bytes=64)
+        sd = const.tile([P, 512], U8, name="sd", align_bytes=64)
         a_codes = const.tile([P, 1024], U32, name="a_codes", align_bytes=64)
         a_scl = const.tile([P, 1024], U8, name="a_scl", align_bytes=64)
         bias = const.tile([P, 2, P], F32, name="bias")
@@ -82,33 +81,11 @@ def tile_gcnfast_t_kernel(tc, h, e, AA_mask, GCW, GCB, out):
             for s in range(a, b):
                 nc.scalar.copy(out=dst[:, s], in_=src[:, s])
 
-        def regroup_pe(u):
-            s0, n = UNITS[u]
-            views(u, 3)
-            bank = psb.tile([P, 2, P, 4], BF16, name="idb", tag="idb")
-            for j in range(4):
-                t = 8 + 2 * j + 1
-                nc.tensor.matmul(
-                    out=bank[:, :, :, j],
-                    lhsT=ident[:],
-                    rhs=raw[:, s0 + 2 : s0 + 4, P * t : P * t + P],
-                    start=True,
-                    stop=True,
-                )
-            nc.scalar.copy(
-                out=grp[(u, 1)][:, 512 * n + 1024 : 512 * n + 2048],
-                in_=bank[:].rearrange("p s d j -> p (s d j)"),
-            )
-
         def regroup(u, q):
             n = UNITS[u][1]
             k = VSHARE[u][q]
-            regroup_v(u, q, 0, k)
-            if q == 3 and u in PE_UNITS:
-                regroup_s(u, q, k, 2)
-                regroup_pe(u)
-            else:
-                regroup_s(u, q, k, n)
+            regroup_s(u, q, 0, n - k)
+            regroup_v(u, q, n - k, n)
 
         def quant_mm(u, t3):
             n = UNITS[u][1]
@@ -144,16 +121,8 @@ def tile_gcnfast_t_kernel(tc, h, e, AA_mask, GCW, GCB, out):
             )
 
         def relu(u):
-            n = UNITS[u][1]
             yf = ys[u][:].rearrange("p s l d -> p (s l d)")
-            g = G_PAIRS if u in G_UNITS else 0
-            if g > 0:
-                nc.gpsimd.tensor_scalar(
-                    out=yf[:, 0 : 256 * g], in0=yf[:, 0 : 256 * g],
-                    scalar1=0.0, scalar2=0.0, op0=ALU.max, op1=ALU.add,
-                )
-            if g < n:
-                nc.scalar.activation(out=yf[:, 256 * g :], in_=yf[:, 256 * g :], func=ACT.Relu)
+            nc.scalar.activation(out=yf, in_=yf, func=ACT.Relu)
 
         def relu_half(u, l):
             nc.scalar.activation(out=ys[u][:, :, l, :], in_=ys[u][:, :, l, :], func=ACT.Relu)
@@ -164,13 +133,17 @@ def tile_gcnfast_t_kernel(tc, h, e, AA_mask, GCW, GCB, out):
                 out=ov[:, s0 : s0 + n, :], in_=ys[u][:].rearrange("p s l d -> p s (l d)")
             )
 
-        nc.vector.memset(ga[:].bitcast(I32), 0)
+        nc.vector.memset(a_codes[:].bitcast(I32), 0)
+        nc.vector.memset(sd[:].bitcast(I32), 0)
         make_identity(nc, ident[:])
-        nc.sync.dma_start(out=gcw[:], in_=GCW)
-        nc.sync.dma_start(out=msk[:], in_=AA_mask)
-        nc.sync.dma_start(out=gcb[:], in_=GCB)
+        nc.gpsimd.memset(a_scl[:], 1)
+        nc.sync.dma_start(out=gcw[:, 0:512], in_=GCW[:, 0:512])
+        nc.sync.dma_start(out=msk[:, 0:512], in_=AA_mask[:, 0:512])
         nc.sync.dma_start(out=raw[:, 0, 0:1024], in_=hv[:, 0, 0:1024])
+        nc.sync.dma_start(out=gcw[:, 512:1024], in_=GCW[:, 512:1024])
+        nc.sync.dma_start(out=msk[:, 512:1024], in_=AA_mask[:, 512:1024])
         nc.sync.dma_start(out=raw[:, 0, 1024:2048], in_=hv[:, 0, 1024:2048])
+        nc.sync.dma_start(out=gcb[:], in_=GCB)
         for a, b in LOADS:
             nc.sync.dma_start(out=raw[:, a:b, :], in_=hv[:, a:b, :])
 
@@ -183,32 +156,55 @@ def tile_gcnfast_t_kernel(tc, h, e, AA_mask, GCW, GCB, out):
             in_=perm[:].rearrange("p (l m) -> p l m", l=2).unsqueeze(2).to_broadcast([P, 2, 2, 64]),
         )
 
-        def pieces(s):
-            regroup_v(0, 0, s, s + 1)
-            regroup_s(0, 1, s, s + 1)
-            regroup_v(0, 2, s, s + 1)
-            regroup_s(0, 3, s, s + 1)
+        def pieces(s, tiles):
+            for q in tiles:
+                if q in V_HEAD[s]:
+                    regroup_v(0, q, s, s + 1)
+                else:
+                    regroup_s(0, q, s, s + 1)
 
-        nc.vector.tensor_tensor(out=pa[:], in0=gcw[:], in1=msk[:], op=ALU.mult)
-        pav = pa[:].rearrange("p (u e c) -> p u e c", u=8, e=2, c=64)
-        pbv = pb[:].rearrange("p (u e c) -> p u e c", u=8, e=2, c=64)
-        for ee in range(2):
-            nc.vector.tensor_copy(out=pbv[:, :, ee, :], in_=pav[:, :, 1 - ee, :])
-        psx = []
-        psz = []
-        for t3 in range(2):
-            px = psa.tile([P, 4, P], BF16, name="px", tag="acc")
-            for j in range(4):
-                u = 4 * t3 + j
-                nc.tensor.transpose(out=px[:, j, :], in_=pa[:, P * u : P * u + P], identity=perm[:])
-            psx.append(px)
-        for t3 in range(2):
-            pz = psa.tile([P, 4, P], BF16, name="pz", tag="acc")
-            for j in range(4):
-                u = 4 * t3 + j
-                nc.tensor.transpose(out=pz[:, j, :], in_=pb[:, P * u : P * u + P], identity=perm[:])
-            psz.append(pz)
-        bps = psb.tile([P, 2, P], F32, name="bps", tag="idb")
+        banks = []
+
+        def mask_and_transpose(t3):
+            lo = 512 * t3
+            nc.vector.tensor_tensor(
+                out=pa2[:, 8 * t3 : 8 * t3 + 8, :, :],
+                in0=gcw[:, lo : lo + 512].rearrange("p (t c) -> p t c", c=64).unsqueeze(2).to_broadcast([P, 8, 2, 64]),
+                in1=msk[:, lo : lo + 512].rearrange("p (t c) -> p t c", c=64).unsqueeze(2).to_broadcast([P, 8, 2, 64]),
+                op=ALU.mult,
+            )
+            bank = psa.tile([P, 8, P], BF16, name="at", tag="acc")
+            for tt in range(8):
+                nc.tensor.transpose(
+                    out=bank[:, tt, :],
+                    in_=pa2[:, 8 * t3 + tt, :, :].rearrange("p b c -> p (b c)"),
+                    identity=perm[:],
+                )
+            banks.append(bank)
+
+        def a_views(t3):
+            dst = gd[:, 1024 * t3 : 1024 * t3 + 1024].rearrange("p (e w j) -> p e w j", e=2, w=P, j=4)
+            src = banks[t3][:].rearrange("p (j e) w -> p e w j", j=4, e=2)
+            return dst, src
+
+        mask_and_transpose(0)
+        pieces(0, (0, 1))
+        mask_and_transpose(1)
+        pieces(0, (2, 3))
+        dst, src = a_views(0)
+        nc.vector.tensor_scalar_max(out=dst, in0=src, scalar1=0.0)
+        dst, src = a_views(1)
+        nc.scalar.activation(out=dst, in_=src, func=ACT.Relu)
+        pieces(1, (0, 1, 2, 3))
+        nc.vector.quantize_mx(out=cd[:].bitcast(FP8X4), scales=sd[:], in_=gd[:])
+        acv = a_codes[:].bitcast(I32).rearrange("p (g b m) -> p g b m", g=8, b=2, m=64)
+        cdv = cd[:].bitcast(I32).rearrange("p (g m) -> p g m", g=8, m=64)
+        asv = a_scl[:].bitcast(I32).rearrange("p (g b m) -> p g b m", g=8, b=2, m=16)
+        sdv = sd[:].bitcast(I32).rearrange("p (g m) -> p g m", g=8, m=16)
+        for b1 in range(2):
+            nc.vector.tensor_copy(out=acv[64 * b1 : 64 * b1 + 64, :, b1, :], in_=cdv[64 * b1 : 64 * b1 + 64])
+            nc.vector.tensor_copy(out=asv[64 * b1 : 64 * b1 + 64, :, b1, :], in_=sdv[64 * b1 : 64 * b1 + 64])
+        bps = psb.tile([P, 2, P], F32, name="bps", tag="bps")
         for l in range(2):
             nc.tensor.matmul(
                 out=bps[:, l, :],
@@ -217,46 +213,22 @@ def tile_gcnfast_t_kernel(tc, h, e, AA_mask, GCW, GCB, out):
                 start=True,
                 stop=True,
             )
-        gav = ga[:].rearrange("p (q l b m j) -> p q l b m j", q=4, l=2, b=2, m=64, j=4)
-
-        def pview(ps, lo, hi):
-            return ps[lo:hi].rearrange("p j (l m) -> p l m j", l=2)
-
-        def evac(ps, t3, qlo, qhi):
-            nc.vector.tensor_scalar_max(
-                out=gav[0:64, 2 * t3 + qlo, :, 0, :, :], in0=pview(ps[t3], 0, 64), scalar1=0.0
-            )
-            nc.scalar.activation(
-                out=gav[64:128, 2 * t3 + qhi, :, 1, :, :], in_=pview(ps[t3], 64, 128), func=ACT.Relu
-            )
-
-        pieces(0)
-        evac(psx, 0, 0, 1)
-        pieces(1)
-        evac(psx, 1, 0, 1)
-        evac(psz, 0, 1, 0)
-        pieces(2)
-        evac(psz, 1, 1, 0)
         nc.vector.tensor_copy(out=bias[:], in_=bps[:])
-        pieces(3)
-        nc.vector.quantize_mx(out=a_codes[:].bitcast(FP8X4), scales=a_scl[:], in_=ga[:])
+        pieces(2, (0, 1, 2, 3))
+        pieces(3, (0, 1, 2, 3))
         quant_mm(0, 0)
+        quant_mm(0, 1)
 
         for u in range(1, nu):
-            regroup(u, 0)
-            regroup(u, 1)
-            if u == nu - 1:
-                regroup(u, 2)
-                regroup(u, 3)
             if u >= 2:
                 add(u - 2, 0)
                 add(u - 2, 1)
+                quant_mm(u - 1, 1)
+            for q in range(4):
+                regroup(u, q)
+            if u >= 2:
                 relu(u - 2)
                 store(u - 2)
-            quant_mm(u - 1, 1)
-            if u < nu - 1:
-                regroup(u, 2)
-                regroup(u, 3)
             quant_mm(u, 0)
 
         quant_mm(nu - 1, 1)

@@ -16,7 +16,8 @@ P = 128
 FLOPS = 2 * 64 * 128 * 1024 * 128
 UNITS = [(0, 4), (4, 4), (8, 4), (12, 4), (16, 4), (20, 4), (24, 4), (28, 2), (30, 2)]
 LOADS = [(1, 2), (2, 3), (3, 4)] + [(a, a + 2) for a in range(4, 32, 2)]
-VSHARE = [(0, 0, 0, 0)] + [(2, 2, 2, 1)] * 6 + [(1, 1, 1, 1)] * 2
+VSHARE = [(0, 0, 0, 0)] + [(2, 2, 2, 1), (2, 1, 2, 1)] * 3 + [(1, 1, 1, 1)] * 2
+PE_UNITS = (1, 2, 3, 4, 5, 6)
 V_HEAD = [(0, 2), (0, 2), (0, 2), (0, 2)]
 
 
@@ -81,10 +82,34 @@ def tile_gcnfast_t_kernel(tc, h, e, AA_mask, GCW, GCB, out):
             for s in range(a, b):
                 nc.scalar.copy(out=dst[:, s], in_=src[:, s])
 
+        idb = {}
+
+        def pe_regroup(u):
+            if u not in PE_UNITS:
+                return
+            s0 = UNITS[u][0]
+            bank = psb.tile([P, 2, P, 4], BF16, name="idb", tag="idb")
+            rv = raw[:, s0 : s0 + 2, :].rearrange("p s (a j e d) -> p s a j e d", a=2, j=4, e=2, d=P)
+            for s in range(2):
+                for jp in range(2):
+                    nc.tensor.matmul(
+                        out=bank[:, s, :, 2 * jp : 2 * jp + 2],
+                        lhsT=ident[:],
+                        rhs=rv[:, s, 0, 2 * jp : 2 * jp + 2, 0, :].rearrange("p j d -> p d j"),
+                        start=True,
+                        stop=True,
+                    )
+            idb[u] = bank
+
         def regroup(u, q):
             n = UNITS[u][1]
             k = VSHARE[u][q]
-            regroup_s(u, q, 0, n - k)
+            first = 0
+            if q == 0 and u in PE_UNITS:
+                views(u, q)
+                nc.scalar.copy(out=grp[(u, 0)][:, 0:1024], in_=idb[u][:].rearrange("p s d j -> p (s d j)"))
+                first = 2
+            regroup_s(u, q, first, n - k)
             regroup_v(u, q, n - k, n)
 
         def quant_mm(u, t3):
@@ -216,6 +241,7 @@ def tile_gcnfast_t_kernel(tc, h, e, AA_mask, GCW, GCB, out):
         nc.vector.tensor_copy(out=bias[:], in_=bps[:])
         pieces(2, (0, 1, 2, 3))
         pieces(3, (0, 1, 2, 3))
+        pe_regroup(1)
         quant_mm(0, 0)
         quant_mm(0, 1)
 
@@ -226,6 +252,8 @@ def tile_gcnfast_t_kernel(tc, h, e, AA_mask, GCW, GCB, out):
                 quant_mm(u - 1, 1)
             for q in range(4):
                 regroup(u, q)
+                if q == 0:
+                    pe_regroup(u + 1)
             if u >= 2:
                 relu(u - 2)
                 store(u - 2)
@@ -239,5 +267,5 @@ def tile_gcnfast_t_kernel(tc, h, e, AA_mask, GCW, GCB, out):
         add(nu - 1, 0)
         relu_half(nu - 1, 0)
         add(nu - 1, 1)
-        relu_half(nu - 1, 1)
+        nc.vector.tensor_scalar_max(out=ys[nu - 1][:, :, 1, :], in0=ys[nu - 1][:, :, 1, :], scalar1=0.0)
         store(nu - 1)

@@ -15,9 +15,9 @@ ACT = mybir.ActivationFunctionType
 P = 128
 FLOPS = 2 * 64 * 128 * 1024 * 128
 UNITS = [(0, 4), (4, 4), (8, 4), (12, 4), (16, 4), (20, 4), (24, 4), (28, 2), (30, 2)]
-LOADS = [(1, 2), (2, 3), (3, 4)] + [(a, a + 2) for a in range(4, 32, 2)]
-VSHARE = [(0, 0, 0, 0)] + [(2, 2, 2, 1), (2, 1, 2, 1)] * 3 + [(1, 1, 1, 1)] * 2
-PE_UNITS = (1, 2, 3, 4, 5, 6)
+LOADS = [(a, a + 1) for a in range(1, 12)] + [(a, a + 2) for a in range(12, 32, 2)]
+VSHARE = [(0, 0, 0, 0)] * 3 + [(2, 2, 2, 1)] * 4 + [(1, 1, 1, 1)] * 2
+BY_ARRIVAL = {1: (4, 4), 2: (4, 3)}
 V_HEAD = [(0, 2), (0, 2), (0, 2), (0, 2)]
 
 
@@ -82,35 +82,22 @@ def tile_gcnfast_t_kernel(tc, h, e, AA_mask, GCW, GCB, out):
             for s in range(a, b):
                 nc.scalar.copy(out=dst[:, s], in_=src[:, s])
 
-        idb = {}
-
-        def pe_regroup(u):
-            if u not in PE_UNITS:
-                return
-            s0 = UNITS[u][0]
-            bank = psb.tile([P, 2, P, 4], BF16, name="idb", tag="idb")
-            rv = raw[:, s0 : s0 + 2, :].rearrange("p s (a j e d) -> p s a j e d", a=2, j=4, e=2, d=P)
-            for s in range(2):
-                for jp in range(2):
-                    nc.tensor.matmul(
-                        out=bank[:, s, :, 2 * jp : 2 * jp + 2],
-                        lhsT=ident[:],
-                        rhs=rv[:, s, 0, 2 * jp : 2 * jp + 2, 0, :].rearrange("p j d -> p d j"),
-                        start=True,
-                        stop=True,
-                    )
-            idb[u] = bank
-
         def regroup(u, q):
             n = UNITS[u][1]
             k = VSHARE[u][q]
-            first = 0
-            if q == 0 and u in PE_UNITS:
-                views(u, q)
-                nc.scalar.copy(out=grp[(u, 0)][:, 0:1024], in_=idb[u][:].rearrange("p s d j -> p (s d j)"))
-                first = 2
-            regroup_s(u, q, first, n - k)
+            regroup_s(u, q, 0, n - k)
             regroup_v(u, q, n - k, n)
+
+        def regroup_by_arrival(u):
+            n = UNITS[u][1]
+            v0, v2 = BY_ARRIVAL[u]
+            for a in range(0, n, 2):
+                regroup_v(u, 0, a, min(a + 2, v0))
+                regroup_v(u, 2, a, min(a + 2, v2))
+                regroup_s(u, 1, a, a + 2)
+                regroup_s(u, 3, a, a + 2)
+                regroup_s(u, 0, max(a, v0), a + 2)
+                regroup_s(u, 2, max(a, v2), a + 2)
 
         def quant_mm(u, t3):
             n = UNITS[u][1]
@@ -241,7 +228,6 @@ def tile_gcnfast_t_kernel(tc, h, e, AA_mask, GCW, GCB, out):
         nc.vector.tensor_copy(out=bias[:], in_=bps[:])
         pieces(2, (0, 1, 2, 3))
         pieces(3, (0, 1, 2, 3))
-        pe_regroup(1)
         quant_mm(0, 0)
         quant_mm(0, 1)
 
@@ -250,10 +236,11 @@ def tile_gcnfast_t_kernel(tc, h, e, AA_mask, GCW, GCB, out):
                 add(u - 2, 0)
                 add(u - 2, 1)
                 quant_mm(u - 1, 1)
-            for q in range(4):
-                regroup(u, q)
-                if q == 0:
-                    pe_regroup(u + 1)
+            if u in BY_ARRIVAL:
+                regroup_by_arrival(u)
+            else:
+                for q in range(4):
+                    regroup(u, q)
             if u >= 2:
                 relu(u - 2)
                 store(u - 2)

@@ -15,9 +15,8 @@ ACT = mybir.ActivationFunctionType
 P = 128
 FLOPS = 2 * 64 * 128 * 1024 * 128
 UNITS = [(0, 4), (4, 4), (8, 4), (12, 4), (16, 4), (20, 4), (24, 4), (28, 2), (30, 2)]
-LOADS = [(a, a + 1) for a in range(1, 12)] + [(a, a + 2) for a in range(12, 32, 2)]
-VSHARE = [(0, 0, 0, 0)] * 3 + [(2, 2, 2, 1)] * 4 + [(1, 1, 1, 1)] * 2
-BY_ARRIVAL = {1: (4, 4), 2: (4, 3)}
+LOADS = [(1, 2), (2, 3), (3, 4)] + [(a, a + 2) for a in range(4, 32, 2)]
+VSHARE = [(0, 0, 0, 0)] + [(2, 2, 2, 2), (2, 2, 2, 1)] * 3 + [(1, 1, 1, 1)] * 2
 V_HEAD = [(0, 2), (0, 2), (0, 2), (0, 2)]
 
 
@@ -87,17 +86,6 @@ def tile_gcnfast_t_kernel(tc, h, e, AA_mask, GCW, GCB, out):
             k = VSHARE[u][q]
             regroup_s(u, q, 0, n - k)
             regroup_v(u, q, n - k, n)
-
-        def regroup_by_arrival(u):
-            n = UNITS[u][1]
-            v0, v2 = BY_ARRIVAL[u]
-            for a in range(0, n, 2):
-                regroup_v(u, 0, a, min(a + 2, v0))
-                regroup_v(u, 2, a, min(a + 2, v2))
-                regroup_s(u, 1, a, a + 2)
-                regroup_s(u, 3, a, a + 2)
-                regroup_s(u, 0, max(a, v0), a + 2)
-                regroup_s(u, 2, max(a, v2), a + 2)
 
         def quant_mm(u, t3):
             n = UNITS[u][1]
@@ -236,11 +224,8 @@ def tile_gcnfast_t_kernel(tc, h, e, AA_mask, GCW, GCB, out):
                 add(u - 2, 0)
                 add(u - 2, 1)
                 quant_mm(u - 1, 1)
-            if u in BY_ARRIVAL:
-                regroup_by_arrival(u)
-            else:
-                for q in range(4):
-                    regroup(u, q)
+            for q in range(4):
+                regroup(u, q)
             if u >= 2:
                 relu(u - 2)
                 store(u - 2)
@@ -254,5 +239,5 @@ def tile_gcnfast_t_kernel(tc, h, e, AA_mask, GCW, GCB, out):
         add(nu - 1, 0)
         relu_half(nu - 1, 0)
         add(nu - 1, 1)
-        nc.vector.tensor_scalar_max(out=ys[nu - 1][:, :, 1, :], in0=ys[nu - 1][:, :, 1, :], scalar1=0.0)
+        relu_half(nu - 1, 1)
         store(nu - 1)

from contextlib import ExitStack

import concourse.mybir as mybir
from concourse.masks import make_identity

BF16 = mybir.dt.bfloat16
F32 = mybir.dt.float32
U32 = mybir.dt.uint32
U8 = mybir.dt.uint8
I32 = mybir.dt.int32
FP8X4 = mybir.dt.float8_e4m3fn_x4
ALU = mybir.AluOpType
ACT = mybir.ActivationFunctionType

P = 128
FLOPS = 2 * 64 * 128 * 1024 * 128
UNITS = [(0, 4), (4, 4), (8, 4), (12, 4), (16, 4), (20, 4), (24, 4), (28, 2), (30, 2)]
LOADS = [(1, 2), (2, 3), (3, 4)] + [(a, a + 2) for a in range(4, 32, 2)]
VSHARE = [(0, 0, 0, 0)] + [(2, 2, 2, 2), (2, 2, 2, 1)] * 3 + [(1, 1, 1, 1)] * 2
V_HEAD = [(0, 2), (0, 2), (0, 2), (0, 2)]


def tile_gcnfast_t_kernel(tc, h, e, AA_mask, GCW, GCB, out):
    nc = tc.nc
    nu = len(UNITS)
    with ExitStack() as ctx:
        ctx.enter_context(tc.manual_schedule())
        const = ctx.enter_context(tc.tile_pool(name="const", bufs=1))
        rawp = ctx.enter_context(tc.tile_pool(name="rawp", bufs=1))
        grpp = ctx.enter_context(tc.tile_pool(name="grpp", bufs=4))
        codp = ctx.enter_context(tc.tile_pool(name="codp", bufs=3))
        yp = ctx.enter_context(tc.tile_pool(name="yp", bufs=8))
        psa = ctx.enter_context(tc.psum_pool(name="psa", bufs=6))
        psb = ctx.enter_context(tc.psum_pool(name="psb", bufs=1))

        hv = h.rearrange("b c t d -> (b c t d)").rearrange("(s m r) -> m s r", m=P, r=2048)
        ov = out.rearrange("b s t d -> (b s t d)").rearrange("(s m r) -> m s r", m=P, r=256)

        ident = const.tile([P, P], BF16, name="ident")
        perm = const.tile([P, P], BF16, name="perm")
        sel = const.tile([P, 2, 2, 64], BF16, name="sel")
        gcw = const.tile([P, 1024], BF16, name="gcw")
        msk = const.tile([P, 1024], BF16, name="msk")
        gcb = const.tile([P, P], BF16, name="gcb")
        pa2 = const.tile([P, 16, 2, 64], BF16, name="pa2")
        gd = const.tile([P, 2048], BF16, name="gd", align_bytes=64)
        cd = const.tile([P, 512], U32, name="cd", align_bytes=64)
        sd = const.tile([P, 512], U8, name="sd", align_bytes=64)
        a_codes = const.tile([P, 1024], U32, name="a_codes", align_bytes=64)
        a_scl = const.tile([P, 1024], U8, name="a_scl", align_bytes=64)
        bias = const.tile([P, 2, P], F32, name="bias")
        raw = rawp.tile([P, 32, 2048], BF16, name="raw")

        grp = {}
        acc = {}
        ys = {}

        def views(u, q):
            s0, n = UNITS[u]
            t3, t0 = q // 2, q % 2
            if (u, t3) not in grp:
                grp[(u, t3)] = grpp.tile([P, 1024 * n], BF16, name="grp", tag="grp", align_bytes=64)
            rv = raw[:, s0 : s0 + n, :].rearrange(
                "p s (a j e c i) -> p s a j e c i", a=2, j=4, e=2, c=32, i=4
            )
            src = rv[:, :, t3, :, t0, :, :].rearrange("p s j c i -> p s c j i")
            dst = grp[(u, t3)][:, 512 * n * t0 : 512 * n * (t0 + 1)].rearrange(
                "p (s c i j) -> p s c j i", s=n, c=32, i=4, j=4
            )
            return src, dst

        def regroup_v(u, q, a, b):
            src, dst = views(u, q)
            if b - a == 1:
                nc.vector.tensor_copy(out=dst[:, a], in_=src[:, a])
            elif b > a:
                nc.vector.tensor_copy(out=dst[:, a:b], in_=src[:, a:b])

        def regroup_s(u, q, a, b):
            src, dst = views(u, q)
            for s in range(a, b):
                nc.scalar.copy(out=dst[:, s], in_=src[:, s])

        def regroup(u, q):
            n = UNITS[u][1]
            k = VSHARE[u][q]
            regroup_s(u, q, 0, n - k)
            regroup_v(u, q, n - k, n)

        def quant_mm(u, t3):
            n = UNITS[u][1]
            w = P * n
            cod = codp.tile([P, 2 * w], U32, name="cod", tag="cod", align_bytes=64)
            scl = codp.tile([P, 2 * w], U8, name="scl", tag="scl", align_bytes=64)
            nc.vector.quantize_mx(out=cod[:].bitcast(FP8X4), scales=scl[:], in_=grp[(u, t3)][:])
            for t0 in range(2):
                q = 2 * t3 + t0
                for l in range(2):
                    if q == 0:
                        acc[(u, l)] = psa.tile([P, w], F32, name="acc", tag="acc")
                    col = (q * 2 + l) * P
                    nc.tensor.matmul_mx(
                        out=acc[(u, l)][:],
                        lhsT=a_codes[:, col : col + P].bitcast(FP8X4),
                        lhsT_scale=a_scl[:, col : col + P],
                        rhs=cod[:, w * t0 : w * t0 + w].bitcast(FP8X4),
                        rhs_scale=scl[:, w * t0 : w * t0 + w],
                        start=(q == 0),
                        stop=(q == 3),
                    )

        def add(u, l):
            n = UNITS[u][1]
            if u not in ys:
                ys[u] = yp.tile([P, n, 2, P], F32, name="y", tag="y")
            nc.vector.tensor_tensor(
                out=ys[u][:, :, l, :],
                in0=acc[(u, l)][:].rearrange("p (s d) -> p s d", s=n),
                in1=bias[:, l, :].unsqueeze(1).to_broadcast([P, n, P]),
                op=ALU.add,
            )

        def relu(u):
            yf = ys[u][:].rearrange("p s l d -> p (s l d)")
            nc.scalar.activation(out=yf, in_=yf, func=ACT.Relu)

        def relu_half(u, l):
            nc.scalar.activation(out=ys[u][:, :, l, :], in_=ys[u][:, :, l, :], func=ACT.Relu)

        def store(u):
            s0, n = UNITS[u]
            nc.sync.dma_start(
                out=ov[:, s0 : s0 + n, :], in_=ys[u][:].rearrange("p s l d -> p s (l d)")
            )

        nc.vector.memset(a_codes[:].bitcast(I32), 0)
        nc.vector.memset(sd[:].bitcast(I32), 0)
        make_identity(nc, ident[:])
        nc.gpsimd.memset(a_scl[:], 1)
        nc.sync.dma_start(out=gcw[:, 0:512], in_=GCW[:, 0:512])
        nc.sync.dma_start(out=msk[:, 0:512], in_=AA_mask[:, 0:512])
        nc.sync.dma_start(out=raw[:, 0, 0:1024], in_=hv[:, 0, 0:1024])
        nc.sync.dma_start(out=gcw[:, 512:1024], in_=GCW[:, 512:1024])
        nc.sync.dma_start(out=msk[:, 512:1024], in_=AA_mask[:, 512:1024])
        nc.sync.dma_start(out=raw[:, 0, 1024:2048], in_=hv[:, 0, 1024:2048])
        nc.sync.dma_start(out=gcb[:], in_=GCB)
        for a, b in LOADS:
            nc.sync.dma_start(out=raw[:, a:b, :], in_=hv[:, a:b, :])

        nc.vector.tensor_copy(
            out=perm[:].rearrange("p (l s h) -> p l s h", l=2, s=8, h=8),
            in_=ident[:].rearrange("p (h l s) -> p l s h", h=8, l=2, s=8),
        )
        nc.vector.tensor_copy(
            out=sel[:],
            in_=perm[:].rearrange("p (l m) -> p l m", l=2).unsqueeze(2).to_broadcast([P, 2, 2, 64]),
        )

        def pieces(s, tiles):
            for q in tiles:
                if q in V_HEAD[s]:
                    regroup_v(0, q, s, s + 1)
                else:
                    regroup_s(0, q, s, s + 1)

        banks = []

        def mask_and_transpose(t3):
            lo = 512 * t3
            nc.vector.tensor_tensor(
                out=pa2[:, 8 * t3 : 8 * t3 + 8, :, :],
                in0=gcw[:, lo : lo + 512].rearrange("p (t c) -> p t c", c=64).unsqueeze(2).to_broadcast([P, 8, 2, 64]),
                in1=msk[:, lo : lo + 512].rearrange("p (t c) -> p t c", c=64).unsqueeze(2).to_broadcast([P, 8, 2, 64]),
                op=ALU.mult,
            )
            bank = psa.tile([P, 8, P], BF16, name="at", tag="acc")
            for tt in range(8):
                nc.tensor.transpose(
                    out=bank[:, tt, :],
                    in_=pa2[:, 8 * t3 + tt, :, :].rearrange("p b c -> p (b c)"),
                    identity=perm[:],
                )
            banks.append(bank)

        def a_views(t3):
            dst = gd[:, 1024 * t3 : 1024 * t3 + 1024].rearrange("p (e w j) -> p e w j", e=2, w=P, j=4)
            src = banks[t3][:].rearrange("p (j e) w -> p e w j", j=4, e=2)
            return dst, src

        mask_and_transpose(0)
        pieces(0, (0, 1))
        mask_and_transpose(1)
        pieces(0, (2, 3))
        dst, src = a_views(0)
        nc.vector.tensor_scalar_max(out=dst, in0=src, scalar1=0.0)
        dst, src = a_views(1)
        nc.scalar.activation(out=dst, in_=src, func=ACT.Relu)
        pieces(1, (0, 1, 2, 3))
        nc.vector.quantize_mx(out=cd[:].bitcast(FP8X4), scales=sd[:], in_=gd[:])
        acv = a_codes[:].bitcast(I32).rearrange("p (g b m) -> p g b m", g=8, b=2, m=64)
        cdv = cd[:].bitcast(I32).rearrange("p (g m) -> p g m", g=8, m=64)
        asv = a_scl[:].bitcast(I32).rearrange("p (g b m) -> p g b m", g=8, b=2, m=16)
        sdv = sd[:].bitcast(I32).rearrange("p (g m) -> p g m", g=8, m=16)
        for b1 in range(2):
            nc.vector.tensor_copy(out=acv[64 * b1 : 64 * b1 + 64, :, b1, :], in_=cdv[64 * b1 : 64 * b1 + 64])
            nc.vector.tensor_copy(out=asv[64 * b1 : 64 * b1 + 64, :, b1, :], in_=sdv[64 * b1 : 64 * b1 + 64])
        bps = psb.tile([P, 2, P], F32, name="bps", tag="bps")
        for l in range(2):
            nc.tensor.matmul(
                out=bps[:, l, :],
                lhsT=sel[:, l, :, :].rearrange("p b m -> p (b m)"),
                rhs=gcb[:],
                start=True,
                stop=True,
            )
        nc.vector.tensor_copy(out=bias[:], in_=bps[:])
        pieces(2, (0, 1, 2, 3))
        pieces(3, (0, 1, 2, 3))
        quant_mm(0, 0)
        quant_mm(0, 1)

        for u in range(1, nu):
            if u >= 2:
                add(u - 2, 0)
                add(u - 2, 1)
                quant_mm(u - 1, 1)
            for q in range(4):
                regroup(u, q)
            if u >= 2:
                relu(u - 2)
                store(u - 2)
            quant_mm(u, 0)

        quant_mm(nu - 1, 1)
        add(nu - 2, 0)
        add(nu - 2, 1)
        relu(nu - 2)
        store(nu - 2)
        add(nu - 1, 0)
        relu_half(nu - 1, 0)
        add(nu - 1, 1)
        relu_half(nu - 1, 1)
        store(nu - 1)
